import numpy as np
import ml_dtypes


def mxq(x, axis, fmt="e4m3"):
    dtype, down = {"e4m3": (ml_dtypes.float8_e4m3fn, 7), "e5m2": (ml_dtypes.float8_e5m2, 14)}[fmt]
    v = np.moveaxis(np.asarray(x, np.float32).astype(ml_dtypes.bfloat16).astype(np.float64), axis, -1)
    blocks = v.reshape(v.shape[:-1] + (-1, 32))
    amax = np.abs(blocks).max(-1, keepdims=True)
    byte = np.maximum(np.where(amax > 0, np.frexp(amax)[1] - 1 + 127, 0) - down, 1)
    scale = np.exp2(byte - 127.0)
    codes = (blocks / scale).astype(np.float32).astype(dtype).astype(np.float64)
    return np.moveaxis((codes * scale).reshape(v.shape), -1, axis)


WIDE = False


def mx_kscale(k):
    if not WIDE:
        return np.ones(k)
    levels = np.array([10, -10, 5, -5, 0])
    a = np.random.permutation(np.resize(levels, k // 512 * 4)).reshape(k // 512, 4)
    idx = np.arange(k)
    return np.exp2(a[idx // 512, idx % 128 // 32])


BF16 = ml_dtypes.bfloat16


def bf(x):
    return np.asarray(x, np.float32).astype(BF16)


def f64(x):
    return np.asarray(x).astype(np.float64)


B, M, H_ENC, N, H_DEC = 8192, 512, 512, 128, 128
SNR = 25.0
NOISE_STD = float(np.sqrt(1.0 / (2.0 * 10.0 ** (SNR / 10.0))))


def setup_inputs():
    s = mx_kscale(M)
    t = mx_kscale(H_ENC)
    theta = np.random.uniform(0.3, 1.2)
    return {"x": bf(np.random.standard_normal((B, M)) * s),
            "noise": bf(np.random.standard_normal((B, N)) * NOISE_STD),
            "h": bf(np.array([np.cos(theta), np.sin(theta)])),
            "W1": bf(np.random.standard_normal((H_ENC, M)) / np.sqrt(M) / s[None, :] * t[:, None]),
            "b1": bf(np.random.standard_normal(H_ENC) * 0.3 * t),
            "W2": bf(np.random.standard_normal((N, H_ENC)) / np.sqrt(H_ENC) / t[None, :]),
            "b2": bf(np.random.standard_normal(N) * 0.3)}


def reference(x, noise, h, W1, b1, W2, b2):
    h = f64(h)
    a = np.maximum((mxq(f64(x), 1, "e4m3") @ mxq(f64(W1), 1, "e4m3").T) + f64(b1), 0.0)
    z = (mxq(a, 1, "e4m3") @ mxq(f64(W2), 1, "e4m3").T) + f64(b2)
    scale = np.sqrt(N * 0.5)
    z = scale * z / np.linalg.norm(z, axis=1, keepdims=True)
    zc = z.reshape(B, N // 2, 2)
    yr = zc[..., 0] * h[0] - zc[..., 1] * h[1]
    yi = zc[..., 0] * h[1] + zc[..., 1] * h[0]
    y = np.stack([yr, yi], axis=-1).reshape(B, N)
    return y + f64(noise)

@@ -1,0 +1,285 @@
+from contextlib import ExitStack
+
+import concourse.masks as masks
+import concourse.mybir as mybir
+
+F32 = mybir.dt.float32
+BF16 = mybir.dt.bfloat16
+U32 = mybir.dt.uint32
+U8 = mybir.dt.uint8
+FP8X4 = mybir.dt.float8_e4m3fn_x4
+ACT = mybir.ActivationFunctionType
+ALU = mybir.AluOpType
+
+P = 128
+PACK = 4
+BATCH, D_IN, D_HID, D_OUT = 8192, 512, 512, 128
+CHUNK = 512
+TILES = CHUNK // P
+NCHUNK = BATCH // CHUNK
+ROWS_PER_PARTITION = BATCH // P
+NOISE_TILES = 16
+TINY = 1e-30
+
+FLOPS = 2 * BATCH * D_IN * D_HID + 2 * BATCH * D_HID * D_OUT
+
+
+def tile_channel_net_pa_kernel(tc, x, noise, h, W1, b1, W2, b2, out):
+    nc = tc.nc
+    with ExitStack() as ctx:
+        ctx.enter_context(tc.manual_schedule())
+        keep = ctx.enter_context(tc.tile_pool(name="keep", bufs=1))
+        work = ctx.enter_context(tc.tile_pool(name="work", bufs=3))
+        psum_t = ctx.enter_context(tc.psum_pool(name="psum_t", bufs=2))
+        psum_a = ctx.enter_context(tc.psum_pool(name="psum_a", bufs=PACK))
+        psum_z = ctx.enter_context(tc.psum_pool(name="psum_z", bufs=1))
+        psum_y = ctx.enter_context(tc.psum_pool(name="psum_y", bufs=1))
+
+        h_bf = keep.tile([P, 2], BF16)
+        b1_bf = keep.tile([P, PACK], BF16)
+        b2_bf = keep.tile([P, 1], BF16)
+        with nc.allow_non_contiguous_dma(reason="three vectors of at most 1 KiB"):
+            nc.scalar.dma_start(out=b1_bf[:], in_=b1.rearrange("(q t) -> q t", t=PACK))
+            nc.scalar.dma_start(out=h_bf[:], in_=h.partition_broadcast(P))
+            nc.scalar.dma_start(out=b2_bf[:], in_=b2.rearrange("(q o) -> q o", o=1))
+
+        w1_sb = keep.tile([P, PACK * D_IN], BF16)
+        nc.sync.dma_start(out=w1_sb[:], in_=W1.rearrange("(q t) k -> q (t k)", t=PACK))
+        w2_sb = keep.tile([P, D_HID], BF16)
+        nc.sync.dma_start(out=w2_sb[:], in_=W2)
+        x_cols = x.rearrange("(p r) k -> p (r k)", r=ROWS_PER_PARTITION)
+        noise_rows = noise.rearrange("(p r) n -> p r n", r=ROWS_PER_PARTITION)
+        out_rows = out.rearrange("(p r) n -> p r n", r=ROWS_PER_PARTITION)
+        x_sb = []
+        noise_sb = []
+        for c in range(NCHUNK):
+            x_c = keep.tile([P, TILES * D_IN], BF16, name="x%d" % c)
+            nc.sync.dma_start(out=x_c[:], in_=x_cols[:, c * TILES * D_IN : (c + 1) * TILES * D_IN])
+            x_sb.append(x_c)
+            if (c * TILES) % NOISE_TILES == 0:
+                first = c * TILES
+                n_c = keep.tile([P, NOISE_TILES, D_OUT], BF16, name="noise%d" % c)
+                nc.sync.dma_start(out=n_c[:], in_=noise_rows[:, first : first + NOISE_TILES, :])
+                noise_sb.append(n_c)
+
+        ident = keep.tile([P, P], F32)
+        masks.make_identity(nc, ident[:])
+
+        one = keep.tile([P, 1], F32)
+        nc.vector.memset(one[:], 1.0)
+        one_root = keep.tile([P, 1], F32)
+        nc.scalar.activation(out=one_root[:], in_=one[:], func=ACT.Sqrt)
+
+        b1_f = keep.tile([P, PACK], F32)
+        nc.vector.tensor_copy(out=b1_f[:], in_=b1_bf[:])
+        b2_f = keep.tile([P, 1], F32)
+        nc.vector.tensor_copy(out=b2_f[:], in_=b2_bf[:])
+        h_f = keep.tile([P, 2], F32)
+        nc.vector.tensor_copy(out=h_f[:], in_=h_bf[:])
+        h_re = h_f[:, 0:1]
+        h_im = h_f[:, 1:2]
+        h_im_neg = keep.tile([P, 1], F32)
+        nc.vector.tensor_scalar(
+            out=h_im_neg[:], in0=h_im, scalar1=-1.0, scalar2=None, op0=ALU.mult
+        )
+
+        h_sq = keep.tile([P, 2], F32)
+        nc.vector.tensor_tensor(out=h_sq[:], in0=h_f[:], in1=h_f[:], op=ALU.mult)
+        h_abs2 = keep.tile([P, 1], F32)
+        nc.vector.tensor_tensor(out=h_abs2[:], in0=h_sq[:, 0:1], in1=h_sq[:, 1:2], op=ALU.add)
+        gain2 = keep.tile([P, 1], F32)
+        nc.vector.tensor_scalar(
+            out=gain2[:], in0=h_abs2[:], scalar1=float(D_OUT // 2), scalar2=TINY,
+            op0=ALU.mult, op1=ALU.max,
+        )
+        inv_gain2 = keep.tile([P, 1], F32)
+        nc.vector.reciprocal(out=inv_gain2[:], in_=gain2[:])
+
+        tap_diag = keep.tile([P, P], F32)
+        nc.vector.tensor_scalar(
+            out=tap_diag[:], in0=ident[:], scalar1=h_re, scalar2=None, op0=ALU.mult
+        )
+        tap = keep.tile([P, P], F32)
+        ident_pairs = ident[:].rearrange("n (j e) -> n j e", e=2)
+        diag_pairs = tap_diag[:].rearrange("n (j e) -> n j e", e=2)
+        tap_pairs = tap[:].rearrange("n (j e) -> n j e", e=2)
+        nc.vector.scalar_tensor_tensor(
+            out=tap_pairs[:, :, 0], in0=ident_pairs[:, :, 1], scalar=h_im_neg[:],
+            in1=diag_pairs[:, :, 0], op0=ALU.mult, op1=ALU.add,
+        )
+        nc.vector.scalar_tensor_tensor(
+            out=tap_pairs[:, :, 1], in0=ident_pairs[:, :, 0], scalar=h_im,
+            in1=diag_pairs[:, :, 1], op0=ALU.mult, op1=ALU.add,
+        )
+
+        def transpose_block(rows):
+            words = rows[:].bitcast(F32)
+            banks = []
+            for pair in range(TILES // 2):
+                bank = psum_t.tile([P, 2, 2, P], F32, name="xt", tag="xt")
+                for i in range(2):
+                    for u in range(2):
+                        first = ((2 * pair + i) * 2 + u) * P
+                        nc.tensor.transpose(bank[:, i, u, :], words[:, first : first + P], ident[:])
+                banks.append(bank)
+            return banks
+
+        def interleave_block(banks, grouped):
+            words = grouped[:].bitcast(F32).rearrange("q (i b u) -> q i b u", i=TILES, u=2)
+            for pair in range(TILES // 2):
+                nc.vector.tensor_copy(
+                    out=words[:, 2 * pair : 2 * pair + 2, :, :],
+                    in_=banks[pair][:].rearrange("q i u b -> q i b u"),
+                )
+
+        def quantise(grouped, codes, scales):
+            nc.vector.quantize_mx(out=codes[:].bitcast(FP8X4), scales=scales[:], in_=grouped[:])
+
+        w1_banks = transpose_block(w1_sb)
+        w1_grouped = keep.tile([P, CHUNK * PACK], BF16, align_bytes=64)
+        interleave_block(w1_banks, w1_grouped)
+        w1_codes = keep.tile([P, D_HID], U32, align_bytes=64)
+        w1_scales = keep.tile([P, D_HID], U8, align_bytes=64)
+        quantise(w1_grouped, w1_codes, w1_scales)
+
+        w2_words = w2_sb[:].bitcast(F32).rearrange("n (q u) -> n u q", u=2)
+        w2_bank = psum_t.tile([P, 2, 2, P], F32, name="xt", tag="xt")
+        for u in range(2):
+            nc.tensor.transpose(w2_bank[:, 0, u, :], w2_words[:, u, :], ident[:])
+        w2_grouped = keep.tile([P, D_OUT * PACK], BF16, align_bytes=64)
+        nc.vector.tensor_copy(
+            out=w2_grouped[:].bitcast(F32).rearrange("q (n u) -> q n u", u=2),
+            in_=w2_bank[:, 0, :, :].rearrange("q u n -> q n u"),
+        )
+        w2_codes = keep.tile([P, D_OUT], U32, align_bytes=64)
+        w2_scales = keep.tile([P, D_OUT], U8, align_bytes=64)
+        quantise(w2_grouped, w2_codes, w2_scales)
+
+        x_banks, x_grouped, x_codes, x_scales = {}, {}, {}, {}
+        a_banks, a_planes, a_grouped, a_codes, a_scales = {}, {}, {}, {}, {}
+        zt_bank, zt_sb, y_bank, y_norm, y_scale = {}, {}, {}, {}, {}
+
+        def transpose_x(c):
+            x_banks[c] = transpose_block(x_sb[c])
+
+        def interleave_x(c):
+            x_grouped[c] = work.tile([P, CHUNK * PACK], BF16, name="x_grouped", align_bytes=64)
+            interleave_block(x_banks[c], x_grouped[c])
+
+        def quantise_x(c):
+            x_codes[c] = work.tile([P, CHUNK], U32, name="x_codes", align_bytes=64)
+            x_scales[c] = work.tile([P, CHUNK], U8, name="x_scales", align_bytes=64)
+            quantise(x_grouped[c], x_codes[c], x_scales[c])
+
+        def layer1(c):
+            a_banks[c] = []
+            for t in range(PACK):
+                bank = psum_a.tile([P, CHUNK], F32, name="a_bank", tag="a_bank")
+                units = slice(t * P, (t + 1) * P)
+                nc.tensor.matmul_mx(
+                    out=bank[:],
+                    lhsT=w1_codes[:, units].bitcast(FP8X4),
+                    lhsT_scale=w1_scales[:, units],
+                    rhs=x_codes[c][:].bitcast(FP8X4),
+                    rhs_scale=x_scales[c][:],
+                    start=True,
+                    stop=True,
+                )
+                a_banks[c].append(bank)
+
+        def relu(c):
+            a_planes[c] = work.tile([P, PACK, CHUNK], BF16, name="a_planes")
+            for t in range(PACK):
+                nc.scalar.activation(
+                    out=a_planes[c][:, t, :], in_=a_banks[c][t][:], func=ACT.Relu,
+                    bias=b1_f[:, t : t + 1], scale=1.0,
+                )
+
+        def regroup_a(c):
+            a_grouped[c] = work.tile([P, CHUNK, PACK], BF16, name="a_grouped", align_bytes=64)
+            nc.vector.tensor_copy(
+                out=a_grouped[c][:].rearrange("q (c i) t -> q c t i", i=4),
+                in_=a_planes[c][:].rearrange("q t (c i) -> q c t i", i=4),
+            )
+
+        def quantise_a(c):
+            a_codes[c] = work.tile([P, CHUNK], U32, name="a_codes", align_bytes=64)
+            a_scales[c] = work.tile([P, CHUNK], U8, name="a_scales", align_bytes=64)
+            nc.vector.quantize_mx(
+                out=a_codes[c][:].bitcast(FP8X4),
+                scales=a_scales[c][:],
+                in_=a_grouped[c][:].rearrange("q b t -> q (b t)"),
+            )
+
+        def layer2(c):
+            zt_bank[c] = psum_z.tile([P, CHUNK], F32, name="zt_bank")
+            nc.tensor.matmul_mx(
+                out=zt_bank[c][:],
+                lhsT=w2_codes[:].bitcast(FP8X4),
+                lhsT_scale=w2_scales[:],
+                rhs=a_codes[c][:].bitcast(FP8X4),
+                rhs_scale=a_scales[c][:],
+                start=True,
+                stop=True,
+            )
+
+        def add_b2(c):
+            zt_sb[c] = work.tile([P, CHUNK], F32, name="zt_sb")
+            nc.scalar.activation(
+                out=zt_sb[c][:], in_=zt_bank[c][:], func=ACT.Identity, bias=b2_f[:], scale=1.0
+            )
+
+        def rotate(c):
+            y_bank[c] = psum_y.tile([P, TILES, D_OUT], F32, name="y_bank")
+            for i in range(TILES):
+                nc.tensor.matmul(
+                    out=y_bank[c][:, i, :], lhsT=zt_sb[c][:, i * P : (i + 1) * P], rhs=tap[:],
+                    start=True, stop=True,
+                )
+
+        def row_norms(c):
+            squares = work.tile([P, TILES, D_OUT], BF16, name="squares")
+            sums = work.tile([P, TILES], F32, name="sums")
+            for i in range(TILES):
+                nc.scalar.activation(
+                    out=squares[:, i, :], in_=y_bank[c][:, i, :], func=ACT.Square,
+                    accum_out=sums[:, i : i + 1],
+                )
+            y_norm[c] = work.tile([P, TILES], F32, name="y_norm")
+            nc.scalar.activation(
+                out=y_norm[c][:], in_=sums[:], func=ACT.Sqrt, bias=TINY, scale=inv_gain2[:]
+            )
+
+        def invert_norms(c):
+            y_scale[c] = work.tile([P, TILES], F32, name="y_scale")
+            nc.vector.reciprocal(out=y_scale[c][:], in_=y_norm[c][:])
+
+        def finish(c):
+            result = work.tile([P, TILES, D_OUT], F32, name="result")
+            for i in range(TILES):
+                r = c * TILES + i
+                nc.vector.scalar_tensor_tensor(
+                    out=result[:, i, :], in0=y_bank[c][:, i, :], scalar=y_scale[c][:, i : i + 1],
+                    in1=noise_sb[r // NOISE_TILES][:, r % NOISE_TILES, :],
+                    op0=ALU.mult, op1=ALU.add,
+                )
+            nc.sync.dma_start(out=out_rows[:, c * TILES : (c + 1) * TILES, :], in_=result[:])
+
+        def run(stage, c):
+            if 0 <= c < NCHUNK:
+                stage(c)
+
+        for step in range(-2, NCHUNK + 3):
+            run(transpose_x, step + 2)
+            run(finish, step - 3)
+            run(rotate, step - 2)
+            run(quantise_a, step - 1)
+            run(layer2, step - 1)
+            run(quantise_x, step + 1)
+            run(relu, step)
+            run(layer1, step + 1)
+            run(interleave_x, step + 2)
+            run(row_norms, step - 2)
+            run(add_b2, step - 1)
+            run(regroup_a, step)
+            run(invert_norms, step - 2)

@@ -32,8 +32,7 @@ def tile_channel_net_pa_kernel(tc, x, noise, h, W1, b1, W2, b2, out):
         work = ctx.enter_context(tc.tile_pool(name="work", bufs=3))
         psum_t = ctx.enter_context(tc.psum_pool(name="psum_t", bufs=2))
         psum_a = ctx.enter_context(tc.psum_pool(name="psum_a", bufs=PACK))
-        psum_z = ctx.enter_context(tc.psum_pool(name="psum_z", bufs=1))
-        psum_y = ctx.enter_context(tc.psum_pool(name="psum_y", bufs=1))
+        psum_e = ctx.enter_context(tc.psum_pool(name="psum_e", bufs=1))
 
         h_bf = keep.tile([P, 2], BF16)
         b1_bf = keep.tile([P, PACK], BF16)
@@ -43,10 +42,10 @@ def tile_channel_net_pa_kernel(tc, x, noise, h, W1, b1, W2, b2, out):
             nc.scalar.dma_start(out=h_bf[:], in_=h.partition_broadcast(P))
             nc.scalar.dma_start(out=b2_bf[:], in_=b2.rearrange("(q o) -> q o", o=1))
 
-        w1_sb = keep.tile([P, PACK * D_IN], BF16)
-        nc.sync.dma_start(out=w1_sb[:], in_=W1.rearrange("(q t) k -> q (t k)", t=PACK))
         w2_sb = keep.tile([P, D_HID], BF16)
         nc.sync.dma_start(out=w2_sb[:], in_=W2)
+        w1_sb = keep.tile([P, PACK * D_IN], BF16)
+        nc.sync.dma_start(out=w1_sb[:], in_=W1.rearrange("(q t) k -> q (t k)", t=PACK))
         x_cols = x.rearrange("(p r) k -> p (r k)", r=ROWS_PER_PARTITION)
         noise_rows = noise.rearrange("(p r) n -> p r n", r=ROWS_PER_PARTITION)
         out_rows = out.rearrange("(p r) n -> p r n", r=ROWS_PER_PARTITION)
@@ -124,10 +123,10 @@ def tile_channel_net_pa_kernel(tc, x, noise, h, W1, b1, W2, b2, out):
                 banks.append(bank)
             return banks
 
-        def interleave_block(banks, grouped):
+        def interleave_block(banks, grouped, copies):
             words = grouped[:].bitcast(F32).rearrange("q (i b u) -> q i b u", i=TILES, u=2)
             for pair in range(TILES // 2):
-                nc.vector.tensor_copy(
+                copies[pair](
                     out=words[:, 2 * pair : 2 * pair + 2, :, :],
                     in_=banks[pair][:].rearrange("q i u b -> q i b u"),
                 )
@@ -135,19 +134,12 @@ def tile_channel_net_pa_kernel(tc, x, noise, h, W1, b1, W2, b2, out):
         def quantise(grouped, codes, scales):
             nc.vector.quantize_mx(out=codes[:].bitcast(FP8X4), scales=scales[:], in_=grouped[:])
 
-        w1_banks = transpose_block(w1_sb)
-        w1_grouped = keep.tile([P, CHUNK * PACK], BF16, align_bytes=64)
-        interleave_block(w1_banks, w1_grouped)
-        w1_codes = keep.tile([P, D_HID], U32, align_bytes=64)
-        w1_scales = keep.tile([P, D_HID], U8, align_bytes=64)
-        quantise(w1_grouped, w1_codes, w1_scales)
-
         w2_words = w2_sb[:].bitcast(F32).rearrange("n (q u) -> n u q", u=2)
         w2_bank = psum_t.tile([P, 2, 2, P], F32, name="xt", tag="xt")
         for u in range(2):
             nc.tensor.transpose(w2_bank[:, 0, u, :], w2_words[:, u, :], ident[:])
         w2_grouped = keep.tile([P, D_OUT * PACK], BF16, align_bytes=64)
-        nc.vector.tensor_copy(
+        nc.scalar.copy(
             out=w2_grouped[:].bitcast(F32).rearrange("q (n u) -> q n u", u=2),
             in_=w2_bank[:, 0, :, :].rearrange("q u n -> q n u"),
         )
@@ -164,7 +156,8 @@ def tile_channel_net_pa_kernel(tc, x, noise, h, W1, b1, W2, b2, out):
 
         def interleave_x(c):
             x_grouped[c] = work.tile([P, CHUNK * PACK], BF16, name="x_grouped", align_bytes=64)
-            interleave_block(x_banks[c], x_grouped[c])
+            second = nc.scalar.copy if c % 2 == 1 else nc.vector.tensor_copy
+            interleave_block(x_banks[c], x_grouped[c], (nc.vector.tensor_copy, second))
 
         def quantise_x(c):
             x_codes[c] = work.tile([P, CHUNK], U32, name="x_codes", align_bytes=64)
@@ -212,7 +205,7 @@ def tile_channel_net_pa_kernel(tc, x, noise, h, W1, b1, W2, b2, out):
             )
 
         def layer2(c):
-            zt_bank[c] = psum_z.tile([P, CHUNK], F32, name="zt_bank")
+            zt_bank[c] = psum_e.tile([P, CHUNK], F32, name="zt_bank", tag="end%d" % (c % 2))
             nc.tensor.matmul_mx(
                 out=zt_bank[c][:],
                 lhsT=w2_codes[:].bitcast(FP8X4),
@@ -230,7 +223,7 @@ def tile_channel_net_pa_kernel(tc, x, noise, h, W1, b1, W2, b2, out):
             )
 
         def rotate(c):
-            y_bank[c] = psum_y.tile([P, TILES, D_OUT], F32, name="y_bank")
+            y_bank[c] = psum_e.tile([P, TILES, D_OUT], F32, name="y_bank", tag="end%d" % (c % 2))
             for i in range(TILES):
                 nc.tensor.matmul(
                     out=y_bank[c][:, i, :], lhsT=zt_sb[c][:, i * P : (i + 1) * P], rhs=tap[:],
@@ -269,7 +262,16 @@ def tile_channel_net_pa_kernel(tc, x, noise, h, W1, b1, W2, b2, out):
             if 0 <= c < NCHUNK:
                 stage(c)
 
-        for step in range(-2, NCHUNK + 3):
+        w1_banks = transpose_block(w1_sb)
+        w1_grouped = keep.tile([P, CHUNK * PACK], BF16, align_bytes=64)
+        interleave_block(w1_banks, w1_grouped, (nc.scalar.copy, nc.scalar.copy))
+        transpose_x(0)
+        interleave_x(0)
+        w1_codes = keep.tile([P, D_HID], U32, align_bytes=64)
+        w1_scales = keep.tile([P, D_HID], U8, align_bytes=64)
+        quantise(w1_grouped, w1_codes, w1_scales)
+
+        for step in range(-1, NCHUNK + 3):
             run(transpose_x, step + 2)
             run(finish, step - 3)
             run(rotate, step - 2)

@@ -67,7 +67,7 @@ def tile_channel_net_pa_kernel(tc, x, noise, h, W1, b1, W2, b2, out):
         one = keep.tile([P, 1], F32)
         nc.vector.memset(one[:], 1.0)
         one_root = keep.tile([P, 1], F32)
-        nc.scalar.activation(out=one_root[:], in_=one[:], func=ACT.Sqrt)
+        nc.scalar.activation(out=one_root[:], in_=one[:], func=ACT.Abs_reciprocal_sqrt)
 
         b1_f = keep.tile([P, PACK], F32)
         nc.vector.tensor_copy(out=b1_f[:], in_=b1_bf[:])
@@ -149,7 +149,7 @@ def tile_channel_net_pa_kernel(tc, x, noise, h, W1, b1, W2, b2, out):
 
         x_banks, x_grouped, x_codes, x_scales = {}, {}, {}, {}
         a_banks, a_planes, a_grouped, a_codes, a_scales = {}, {}, {}, {}, {}
-        zt_bank, zt_sb, y_bank, y_norm, y_scale = {}, {}, {}, {}, {}
+        zt_bank, zt_sb, y_bank, y_sums, y_scale = {}, {}, {}, {}, {}
 
         def transpose_x(c):
             x_banks[c] = transpose_block(x_sb[c])
@@ -230,22 +230,21 @@ def tile_channel_net_pa_kernel(tc, x, noise, h, W1, b1, W2, b2, out):
                     start=True, stop=True,
                 )
 
-        def row_norms(c):
+        def sum_squares(c):
             squares = work.tile([P, TILES, D_OUT], BF16, name="squares")
-            sums = work.tile([P, TILES], F32, name="sums")
+            y_sums[c] = work.tile([P, TILES], F32, name="y_sums")
             for i in range(TILES):
                 nc.scalar.activation(
                     out=squares[:, i, :], in_=y_bank[c][:, i, :], func=ACT.Square,
-                    accum_out=sums[:, i : i + 1],
+                    accum_out=y_sums[c][:, i : i + 1],
                 )
-            y_norm[c] = work.tile([P, TILES], F32, name="y_norm")
-            nc.scalar.activation(
-                out=y_norm[c][:], in_=sums[:], func=ACT.Sqrt, bias=TINY, scale=inv_gain2[:]
-            )
 
         def invert_norms(c):
             y_scale[c] = work.tile([P, TILES], F32, name="y_scale")
-            nc.vector.reciprocal(out=y_scale[c][:], in_=y_norm[c][:])
+            nc.scalar.activation(
+                out=y_scale[c][:], in_=y_sums[c][:], func=ACT.Abs_reciprocal_sqrt,
+                bias=TINY, scale=inv_gain2[:],
+            )
 
         def finish(c):
             result = work.tile([P, TILES, D_OUT], F32, name="result")
@@ -281,7 +280,7 @@ def tile_channel_net_pa_kernel(tc, x, noise, h, W1, b1, W2, b2, out):
             run(relu, step)
             run(layer1, step + 1)
             run(interleave_x, step + 2)
-            run(row_norms, step - 2)
+            run(sum_squares, step - 2)
             run(add_b2, step - 1)
-            run(regroup_a, step)
             run(invert_norms, step - 2)
+            run(regroup_a, step)

@@ -279,8 +279,8 @@ def tile_channel_net_pa_kernel(tc, x, noise, h, W1, b1, W2, b2, out):
             run(quantise_x, step + 1)
             run(relu, step)
             run(layer1, step + 1)
-            run(interleave_x, step + 2)
             run(sum_squares, step - 2)
-            run(add_b2, step - 1)
+            run(interleave_x, step + 2)
             run(invert_norms, step - 2)
+            run(add_b2, step - 1)
             run(regroup_a, step)

@@ -111,11 +111,11 @@ def tile_channel_net_pa_kernel(tc, x, noise, h, W1, b1, W2, b2, out):
             in1=diag_pairs[:, :, 1], op0=ALU.mult, op1=ALU.add,
         )
 
-        def transpose_block(rows):
+        def transpose_block(rows, pool, tag):
             words = rows[:].bitcast(F32)
             banks = []
             for pair in range(TILES // 2):
-                bank = psum_t.tile([P, 2, 2, P], F32, name="xt", tag="xt")
+                bank = pool.tile([P, 2, 2, P], F32, name="xt", tag=tag)
                 for i in range(2):
                     for u in range(2):
                         first = ((2 * pair + i) * 2 + u) * P
@@ -152,7 +152,7 @@ def tile_channel_net_pa_kernel(tc, x, noise, h, W1, b1, W2, b2, out):
         zt_bank, zt_sb, y_bank, y_sums, y_scale = {}, {}, {}, {}, {}
 
         def transpose_x(c):
-            x_banks[c] = transpose_block(x_sb[c])
+            x_banks[c] = transpose_block(x_sb[c], psum_t, "xt")
 
         def interleave_x(c):
             x_grouped[c] = work.tile([P, CHUNK * PACK], BF16, name="x_grouped", align_bytes=64)
@@ -261,7 +261,7 @@ def tile_channel_net_pa_kernel(tc, x, noise, h, W1, b1, W2, b2, out):
             if 0 <= c < NCHUNK:
                 stage(c)
 
-        w1_banks = transpose_block(w1_sb)
+        w1_banks = transpose_block(w1_sb, psum_a, "a_bank")
         w1_grouped = keep.tile([P, CHUNK * PACK], BF16, align_bytes=64)
         interleave_block(w1_banks, w1_grouped, (nc.scalar.copy, nc.scalar.copy))
         transpose_x(0)
@@ -272,15 +272,15 @@ def tile_channel_net_pa_kernel(tc, x, noise, h, W1, b1, W2, b2, out):
 
         for step in range(-1, NCHUNK + 3):
             run(transpose_x, step + 2)
+            run(quantise_x, step + 1)
+            run(quantise_a, step - 1)
             run(finish, step - 3)
             run(rotate, step - 2)
-            run(quantise_a, step - 1)
             run(layer2, step - 1)
-            run(quantise_x, step + 1)
             run(relu, step)
             run(layer1, step + 1)
-            run(sum_squares, step - 2)
             run(interleave_x, step + 2)
-            run(invert_norms, step - 2)
+            run(sum_squares, step - 2)
             run(add_b2, step - 1)
+            run(invert_norms, step - 2)
             run(regroup_a, step)

from contextlib import ExitStack

import concourse.masks as masks
import concourse.mybir as mybir

F32 = mybir.dt.float32
BF16 = mybir.dt.bfloat16
U32 = mybir.dt.uint32
U8 = mybir.dt.uint8
FP8X4 = mybir.dt.float8_e4m3fn_x4
ACT = mybir.ActivationFunctionType
ALU = mybir.AluOpType

P = 128
PACK = 4
BATCH, D_IN, D_HID, D_OUT = 8192, 512, 512, 128
CHUNK = 512
TILES = CHUNK // P
NCHUNK = BATCH // CHUNK
ROWS_PER_PARTITION = BATCH // P
NOISE_TILES = 16
TINY = 1e-30

FLOPS = 2 * BATCH * D_IN * D_HID + 2 * BATCH * D_HID * D_OUT


def tile_channel_net_pa_kernel(tc, x, noise, h, W1, b1, W2, b2, out):
    nc = tc.nc
    with ExitStack() as ctx:
        ctx.enter_context(tc.manual_schedule())
        keep = ctx.enter_context(tc.tile_pool(name="keep", bufs=1))
        work = ctx.enter_context(tc.tile_pool(name="work", bufs=3))
        psum_t = ctx.enter_context(tc.psum_pool(name="psum_t", bufs=2))
        psum_a = ctx.enter_context(tc.psum_pool(name="psum_a", bufs=PACK))
        psum_e = ctx.enter_context(tc.psum_pool(name="psum_e", bufs=1))

        h_bf = keep.tile([P, 2], BF16)
        b1_bf = keep.tile([P, PACK], BF16)
        b2_bf = keep.tile([P, 1], BF16)
        with nc.allow_non_contiguous_dma(reason="three vectors of at most 1 KiB"):
            nc.scalar.dma_start(out=b1_bf[:], in_=b1.rearrange("(q t) -> q t", t=PACK))
            nc.scalar.dma_start(out=h_bf[:], in_=h.partition_broadcast(P))
            nc.scalar.dma_start(out=b2_bf[:], in_=b2.rearrange("(q o) -> q o", o=1))

        w2_sb = keep.tile([P, D_HID], BF16)
        nc.sync.dma_start(out=w2_sb[:], in_=W2)
        w1_sb = keep.tile([P, PACK * D_IN], BF16)
        nc.sync.dma_start(out=w1_sb[:], in_=W1.rearrange("(q t) k -> q (t k)", t=PACK))
        x_cols = x.rearrange("(p r) k -> p (r k)", r=ROWS_PER_PARTITION)
        noise_rows = noise.rearrange("(p r) n -> p r n", r=ROWS_PER_PARTITION)
        out_rows = out.rearrange("(p r) n -> p r n", r=ROWS_PER_PARTITION)
        x_sb = []
        noise_sb = []
        for c in range(NCHUNK):
            x_c = keep.tile([P, TILES * D_IN], BF16, name="x%d" % c)
            nc.sync.dma_start(out=x_c[:], in_=x_cols[:, c * TILES * D_IN : (c + 1) * TILES * D_IN])
            x_sb.append(x_c)
            if (c * TILES) % NOISE_TILES == 0:
                first = c * TILES
                n_c = keep.tile([P, NOISE_TILES, D_OUT], BF16, name="noise%d" % c)
                nc.sync.dma_start(out=n_c[:], in_=noise_rows[:, first : first + NOISE_TILES, :])
                noise_sb.append(n_c)

        ident = keep.tile([P, P], F32)
        masks.make_identity(nc, ident[:])

        one = keep.tile([P, 1], F32)
        nc.vector.memset(one[:], 1.0)
        one_root = keep.tile([P, 1], F32)
        nc.scalar.activation(out=one_root[:], in_=one[:], func=ACT.Abs_reciprocal_sqrt)

        b1_f = keep.tile([P, PACK], F32)
        nc.vector.tensor_copy(out=b1_f[:], in_=b1_bf[:])
        b2_f = keep.tile([P, 1], F32)
        nc.vector.tensor_copy(out=b2_f[:], in_=b2_bf[:])
        h_f = keep.tile([P, 2], F32)
        nc.vector.tensor_copy(out=h_f[:], in_=h_bf[:])
        h_re = h_f[:, 0:1]
        h_im = h_f[:, 1:2]
        h_im_neg = keep.tile([P, 1], F32)
        nc.vector.tensor_scalar(
            out=h_im_neg[:], in0=h_im, scalar1=-1.0, scalar2=None, op0=ALU.mult
        )

        h_sq = keep.tile([P, 2], F32)
        nc.vector.tensor_tensor(out=h_sq[:], in0=h_f[:], in1=h_f[:], op=ALU.mult)
        h_abs2 = keep.tile([P, 1], F32)
        nc.vector.tensor_tensor(out=h_abs2[:], in0=h_sq[:, 0:1], in1=h_sq[:, 1:2], op=ALU.add)
        gain2 = keep.tile([P, 1], F32)
        nc.vector.tensor_scalar(
            out=gain2[:], in0=h_abs2[:], scalar1=float(D_OUT // 2), scalar2=TINY,
            op0=ALU.mult, op1=ALU.max,
        )
        inv_gain2 = keep.tile([P, 1], F32)
        nc.vector.reciprocal(out=inv_gain2[:], in_=gain2[:])

        tap_diag = keep.tile([P, P], F32)
        nc.vector.tensor_scalar(
            out=tap_diag[:], in0=ident[:], scalar1=h_re, scalar2=None, op0=ALU.mult
        )
        tap = keep.tile([P, P], F32)
        ident_pairs = ident[:].rearrange("n (j e) -> n j e", e=2)
        diag_pairs = tap_diag[:].rearrange("n (j e) -> n j e", e=2)
        tap_pairs = tap[:].rearrange("n (j e) -> n j e", e=2)
        nc.vector.scalar_tensor_tensor(
            out=tap_pairs[:, :, 0], in0=ident_pairs[:, :, 1], scalar=h_im_neg[:],
            in1=diag_pairs[:, :, 0], op0=ALU.mult, op1=ALU.add,
        )
        nc.vector.scalar_tensor_tensor(
            out=tap_pairs[:, :, 1], in0=ident_pairs[:, :, 0], scalar=h_im,
            in1=diag_pairs[:, :, 1], op0=ALU.mult, op1=ALU.add,
        )

        def transpose_block(rows, pool, tag):
            words = rows[:].bitcast(F32)
            banks = []
            for pair in range(TILES // 2):
                bank = pool.tile([P, 2, 2, P], F32, name="xt", tag=tag)
                for i in range(2):
                    for u in range(2):
                        first = ((2 * pair + i) * 2 + u) * P
                        nc.tensor.transpose(bank[:, i, u, :], words[:, first : first + P], ident[:])
                banks.append(bank)
            return banks

        def interleave_block(banks, grouped, copies):
            words = grouped[:].bitcast(F32).rearrange("q (i b u) -> q i b u", i=TILES, u=2)
            for pair in range(TILES // 2):
                copies[pair](
                    out=words[:, 2 * pair : 2 * pair + 2, :, :],
                    in_=banks[pair][:].rearrange("q i u b -> q i b u"),
                )

        def quantise(grouped, codes, scales):
            nc.vector.quantize_mx(out=codes[:].bitcast(FP8X4), scales=scales[:], in_=grouped[:])

        w2_words = w2_sb[:].bitcast(F32).rearrange("n (q u) -> n u q", u=2)
        w2_bank = psum_t.tile([P, 2, 2, P], F32, name="xt", tag="xt")
        for u in range(2):
            nc.tensor.transpose(w2_bank[:, 0, u, :], w2_words[:, u, :], ident[:])
        w2_grouped = keep.tile([P, D_OUT * PACK], BF16, align_bytes=64)
        nc.scalar.copy(
            out=w2_grouped[:].bitcast(F32).rearrange("q (n u) -> q n u", u=2),
            in_=w2_bank[:, 0, :, :].rearrange("q u n -> q n u"),
        )
        w2_codes = keep.tile([P, D_OUT], U32, align_bytes=64)
        w2_scales = keep.tile([P, D_OUT], U8, align_bytes=64)
        quantise(w2_grouped, w2_codes, w2_scales)

        x_banks, x_grouped, x_codes, x_scales = {}, {}, {}, {}
        a_banks, a_planes, a_grouped, a_codes, a_scales = {}, {}, {}, {}, {}
        zt_bank, zt_sb, y_bank, y_sums, y_scale = {}, {}, {}, {}, {}

        def transpose_x(c):
            x_banks[c] = transpose_block(x_sb[c], psum_t, "xt")

        def interleave_x(c):
            x_grouped[c] = work.tile([P, CHUNK * PACK], BF16, name="x_grouped", align_bytes=64)
            second = nc.scalar.copy if c % 2 == 1 else nc.vector.tensor_copy
            interleave_block(x_banks[c], x_grouped[c], (nc.vector.tensor_copy, second))

        def quantise_x(c):
            x_codes[c] = work.tile([P, CHUNK], U32, name="x_codes", align_bytes=64)
            x_scales[c] = work.tile([P, CHUNK], U8, name="x_scales", align_bytes=64)
            quantise(x_grouped[c], x_codes[c], x_scales[c])

        def layer1(c):
            a_banks[c] = []
            for t in range(PACK):
                bank = psum_a.tile([P, CHUNK], F32, name="a_bank", tag="a_bank")
                units = slice(t * P, (t + 1) * P)
                nc.tensor.matmul_mx(
                    out=bank[:],
                    lhsT=w1_codes[:, units].bitcast(FP8X4),
                    lhsT_scale=w1_scales[:, units],
                    rhs=x_codes[c][:].bitcast(FP8X4),
                    rhs_scale=x_scales[c][:],
                    start=True,
                    stop=True,
                )
                a_banks[c].append(bank)

        def relu(c):
            a_planes[c] = work.tile([P, PACK, CHUNK], BF16, name="a_planes")
            for t in range(PACK):
                nc.scalar.activation(
                    out=a_planes[c][:, t, :], in_=a_banks[c][t][:], func=ACT.Relu,
                    bias=b1_f[:, t : t + 1], scale=1.0,
                )

        def regroup_a(c):
            a_grouped[c] = work.tile([P, CHUNK, PACK], BF16, name="a_grouped", align_bytes=64)
            nc.vector.tensor_copy(
                out=a_grouped[c][:].rearrange("q (c i) t -> q c t i", i=4),
                in_=a_planes[c][:].rearrange("q t (c i) -> q c t i", i=4),
            )

        def quantise_a(c):
            a_codes[c] = work.tile([P, CHUNK], U32, name="a_codes", align_bytes=64)
            a_scales[c] = work.tile([P, CHUNK], U8, name="a_scales", align_bytes=64)
            nc.vector.quantize_mx(
                out=a_codes[c][:].bitcast(FP8X4),
                scales=a_scales[c][:],
                in_=a_grouped[c][:].rearrange("q b t -> q (b t)"),
            )

        def layer2(c):
            zt_bank[c] = psum_e.tile([P, CHUNK], F32, name="zt_bank", tag="end%d" % (c % 2))
            nc.tensor.matmul_mx(
                out=zt_bank[c][:],
                lhsT=w2_codes[:].bitcast(FP8X4),
                lhsT_scale=w2_scales[:],
                rhs=a_codes[c][:].bitcast(FP8X4),
                rhs_scale=a_scales[c][:],
                start=True,
                stop=True,
            )

        def add_b2(c):
            zt_sb[c] = work.tile([P, CHUNK], F32, name="zt_sb")
            nc.scalar.activation(
                out=zt_sb[c][:], in_=zt_bank[c][:], func=ACT.Identity, bias=b2_f[:], scale=1.0
            )

        def rotate(c):
            y_bank[c] = psum_e.tile([P, TILES, D_OUT], F32, name="y_bank", tag="end%d" % (c % 2))
            for i in range(TILES):
                nc.tensor.matmul(
                    out=y_bank[c][:, i, :], lhsT=zt_sb[c][:, i * P : (i + 1) * P], rhs=tap[:],
                    start=True, stop=True,
                )

        def sum_squares(c):
            squares = work.tile([P, TILES, D_OUT], BF16, name="squares")
            y_sums[c] = work.tile([P, TILES], F32, name="y_sums")
            for i in range(TILES):
                nc.scalar.activation(
                    out=squares[:, i, :], in_=y_bank[c][:, i, :], func=ACT.Square,
                    accum_out=y_sums[c][:, i : i + 1],
                )

        def invert_norms(c):
            y_scale[c] = work.tile([P, TILES], F32, name="y_scale")
            nc.scalar.activation(
                out=y_scale[c][:], in_=y_sums[c][:], func=ACT.Abs_reciprocal_sqrt,
                bias=TINY, scale=inv_gain2[:],
            )

        def finish(c):
            result = work.tile([P, TILES, D_OUT], F32, name="result")
            for i in range(TILES):
                r = c * TILES + i
                nc.vector.scalar_tensor_tensor(
                    out=result[:, i, :], in0=y_bank[c][:, i, :], scalar=y_scale[c][:, i : i + 1],
                    in1=noise_sb[r // NOISE_TILES][:, r % NOISE_TILES, :],
                    op0=ALU.mult, op1=ALU.add,
                )
            nc.sync.dma_start(out=out_rows[:, c * TILES : (c + 1) * TILES, :], in_=result[:])

        def run(stage, c):
            if 0 <= c < NCHUNK:
                stage(c)

        w1_banks = transpose_block(w1_sb, psum_a, "a_bank")
        w1_grouped = keep.tile([P, CHUNK * PACK], BF16, align_bytes=64)
        interleave_block(w1_banks, w1_grouped, (nc.scalar.copy, nc.scalar.copy))
        transpose_x(0)
        interleave_x(0)
        w1_codes = keep.tile([P, D_HID], U32, align_bytes=64)
        w1_scales = keep.tile([P, D_HID], U8, align_bytes=64)
        quantise(w1_grouped, w1_codes, w1_scales)

        for step in range(-1, NCHUNK + 3):
            run(transpose_x, step + 2)
            run(quantise_x, step + 1)
            run(quantise_a, step - 1)
            run(finish, step - 3)
            run(rotate, step - 2)
            run(layer2, step - 1)
            run(relu, step)
            run(layer1, step + 1)
            run(interleave_x, step + 2)
            run(sum_squares, step - 2)
            run(add_b2, step - 1)
            run(invert_norms, step - 2)
            run(regroup_a, step)
